import numpy as np
import ml_dtypes

BF16 = ml_dtypes.bfloat16


def bf(x):
    return np.asarray(x, np.float32).astype(BF16)


def f32(x):
    return np.asarray(x, np.float32)


def f64(x):
    return np.asarray(x).astype(np.float64)


def striped(idx):
    return np.tile(idx.reshape(-1, 16).T, (8, 1))


D, M, S, N, A, P = 128, 128, 1024, 128, 4, 2
PW_0E = np.sqrt(0.5)
PW_1O = np.sqrt(1.5)
INV_SQRT3 = 1.0 / np.sqrt(3.0)


def setup_inputs():
    return {"table": bf(np.random.standard_normal((D, S))), "w_up": bf(np.random.standard_normal((D, M))), "tpw": f32(np.random.standard_normal((P * M, N))), "sh": f32(np.random.standard_normal((A, N))), "w_out_s": bf(np.random.standard_normal((M, M))), "w_out_v": bf(np.random.standard_normal((M, M))), "offs": striped(np.random.permutation(np.tile(np.arange(S), 2))[:N])}


def reference(table, w_up, tpw, sh, w_out_s, w_out_v, offs):
    idx = offs[:16].T.reshape(-1)
    ss = f64(w_up).T @ f64(table)[:, idx] / np.sqrt(D)
    t, y = f64(tpw), f64(sh)
    a0 = PW_0E * t[:M] * ss * y[0]
    blocks = [f64(w_out_s).T @ a0 / np.sqrt(P * M)]
    for i in range(1, A):
        a1 = (PW_1O * INV_SQRT3) * t[M:] * ss * y[i]
        blocks.append(f64(w_out_v).T @ a1 / np.sqrt(P * M))
    return np.concatenate(blocks, axis=0)

@@ -1,0 +1,67 @@
+import math
+
+import concourse.mybir as mybir
+
+BF16, F32, U16 = mybir.dt.bfloat16, mybir.dt.float32, mybir.dt.uint16
+MULT = mybir.AluOpType.mult
+COPY = mybir.ActivationFunctionType.Copy
+
+D = 128
+M = 128
+S = 1024
+N = 128
+A = 4
+
+PATH_SCALE = (
+    math.sqrt(0.5) / math.sqrt(D),
+    math.sqrt(1.5) / math.sqrt(3.0) / math.sqrt(D),
+)
+OUT_SCALE = 1.0 / math.sqrt(2 * M)
+
+FLOPS = 2 * D * M * N + A * 2 * M * M * N
+
+
+def tile_maceedgemessageblock_kernel(tc, table, w_up, tpw, sh, w_out_s, w_out_v, offs, out):
+    nc = tc.nc
+    with (
+        tc.tile_pool(name="held", bufs=1) as held,
+        tc.psum_pool(name="psum", bufs=1) as psum,
+    ):
+        offsets = held.tile([128, N // 16], U16, name="offsets")
+        nc.sync.dma_start(offsets[:], offs)
+        w_up_sb = held.tile([D, M], BF16, name="w_up_sb")
+        nc.sync.dma_start(w_up_sb[:], w_up)
+        table_sb = held.tile([D, S], BF16, name="table_sb")
+        nc.sync.dma_start(table_sb[:], table)
+
+        sh_all = held.tile([M, A * N], F32, name="sh_all")
+        nc.scalar.dma_start(sh_all[:], sh.rearrange("a j -> (a j)").partition_broadcast(M))
+        tpw_sb = [held.tile([M, N], F32, name=f"tpw_sb{path}") for path in range(2)]
+        for path in range(2):
+            nc.scalar.dma_start(tpw_sb[path][:], tpw[path * M : (path + 1) * M, :])
+
+        w_out_sb = [held.tile([M, M], BF16, name=f"w_out_sb{path}") for path in range(2)]
+        nc.gpsimd.dma_start(w_out_sb[0][:], w_out_s)
+        nc.gpsimd.dma_start(w_out_sb[1][:], w_out_v)
+
+        factor = held.tile([M, A * N], F32, name="factor")
+        for i in range(A):
+            path = min(i, 1)
+            block = slice(i * N, (i + 1) * N)
+            nc.vector.scalar_tensor_tensor(
+                factor[:, block], tpw_sb[path][:], PATH_SCALE[path], sh_all[:, block], MULT, MULT
+            )
+
+        ss_raw = psum.tile([M, N], F32, name="ss_raw")
+        nc.tensor.matmul(ss_raw[:], w_up_sb[:], table_sb[:].indirect(offsets[:]), start=True, stop=True)
+
+        for i in range(A):
+            path = min(i, 1)
+            block = slice(i * N, (i + 1) * N)
+            a_i = held.tile([M, N], BF16, name=f"a_{i}")
+            nc.vector.tensor_tensor(a_i[:], ss_raw[:], factor[:, block], MULT)
+            mixed = psum.tile([M, N], F32, name=f"mixed{i}")
+            nc.tensor.matmul(mixed[:], w_out_sb[path][:], a_i[:], start=True, stop=True)
+            message = held.tile([M, N], F32, name=f"message{i}")
+            nc.scalar.activation(message[:], mixed[:], COPY, scale=OUT_SCALE)
+            nc.sync.dma_start(out[i * M : (i + 1) * M, :], message[:])

@@ -41,8 +41,8 @@ def tile_maceedgemessageblock_kernel(tc, table, w_up, tpw, sh, w_out_s, w_out_v,
             nc.scalar.dma_start(tpw_sb[path][:], tpw[path * M : (path + 1) * M, :])
 
         w_out_sb = [held.tile([M, M], BF16, name=f"w_out_sb{path}") for path in range(2)]
-        nc.gpsimd.dma_start(w_out_sb[0][:], w_out_s)
-        nc.gpsimd.dma_start(w_out_sb[1][:], w_out_v)
+        nc.sync.dma_start(w_out_sb[0][:], w_out_s)
+        nc.scalar.dma_start(w_out_sb[1][:], w_out_v)
 
         factor = held.tile([M, A * N], F32, name="factor")
         for i in range(A):

@@ -27,29 +27,31 @@ def tile_maceedgemessageblock_kernel(tc, table, w_up, tpw, sh, w_out_s, w_out_v,
         tc.tile_pool(name="held", bufs=1) as held,
         tc.psum_pool(name="psum", bufs=1) as psum,
     ):
-        offsets = held.tile([128, N // 16], U16, name="offsets")
-        nc.sync.dma_start(offsets[:], offs)
-        w_up_sb = held.tile([D, M], BF16, name="w_up_sb")
-        nc.sync.dma_start(w_up_sb[:], w_up)
         table_sb = held.tile([D, S], BF16, name="table_sb")
         nc.sync.dma_start(table_sb[:], table)
+        w_up_sb = held.tile([D, M], BF16, name="w_up_sb")
+        nc.sync.dma_start(w_up_sb[:], w_up)
+        offsets = held.tile([128, N // 16], U16, name="offsets")
+        nc.sync.dma_start(offsets[:], offs)
 
-        sh_all = held.tile([M, A * N], F32, name="sh_all")
-        nc.scalar.dma_start(sh_all[:], sh.rearrange("a j -> (a j)").partition_broadcast(M))
-        tpw_sb = [held.tile([M, N], F32, name=f"tpw_sb{path}") for path in range(2)]
-        for path in range(2):
-            nc.scalar.dma_start(tpw_sb[path][:], tpw[path * M : (path + 1) * M, :])
+        tpw_sb = held.tile([M, 2, N], F32, name="tpw_sb")
+        nc.scalar.dma_start(tpw_sb[:], tpw.rearrange("(path u) j -> u path j", path=2))
+        sh_all = held.tile([M, A, N], F32, name="sh_all")
+        for first in range(0, A, 2):
+            nc.scalar.dma_start(
+                sh_all[:, first : first + 2, :],
+                sh[first : first + 2, :].unsqueeze(0).broadcast_to([M, 2, N]),
+            )
 
         w_out_sb = [held.tile([M, M], BF16, name=f"w_out_sb{path}") for path in range(2)]
         nc.sync.dma_start(w_out_sb[0][:], w_out_s)
         nc.scalar.dma_start(w_out_sb[1][:], w_out_v)
 
-        factor = held.tile([M, A * N], F32, name="factor")
+        factor = held.tile([M, A, N], F32, name="factor")
         for i in range(A):
             path = min(i, 1)
-            block = slice(i * N, (i + 1) * N)
             nc.vector.scalar_tensor_tensor(
-                factor[:, block], tpw_sb[path][:], PATH_SCALE[path], sh_all[:, block], MULT, MULT
+                factor[:, i, :], tpw_sb[:, path, :], PATH_SCALE[path], sh_all[:, i, :], MULT, MULT
             )
 
         ss_raw = psum.tile([M, N], F32, name="ss_raw")
@@ -57,9 +59,8 @@ def tile_maceedgemessageblock_kernel(tc, table, w_up, tpw, sh, w_out_s, w_out_v,
 
         for i in range(A):
             path = min(i, 1)
-            block = slice(i * N, (i + 1) * N)
             a_i = held.tile([M, N], BF16, name=f"a_{i}")
-            nc.vector.tensor_tensor(a_i[:], ss_raw[:], factor[:, block], MULT)
+            nc.vector.tensor_tensor(a_i[:], ss_raw[:], factor[:, i, :], MULT)
             mixed = psum.tile([M, N], F32, name=f"mixed{i}")
             nc.tensor.matmul(mixed[:], w_out_sb[path][:], a_i[:], start=True, stop=True)
             message = held.tile([M, N], F32, name=f"message{i}")

@@ -27,40 +27,39 @@ def tile_maceedgemessageblock_kernel(tc, table, w_up, tpw, sh, w_out_s, w_out_v,
         tc.tile_pool(name="held", bufs=1) as held,
         tc.psum_pool(name="psum", bufs=1) as psum,
     ):
-        table_sb = held.tile([D, S], BF16, name="table_sb")
-        nc.sync.dma_start(table_sb[:], table)
         w_up_sb = held.tile([D, M], BF16, name="w_up_sb")
         nc.sync.dma_start(w_up_sb[:], w_up)
         offsets = held.tile([128, N // 16], U16, name="offsets")
         nc.sync.dma_start(offsets[:], offs)
+        table_sb = held.tile([D, S], BF16, name="table_sb")
+        nc.sync.dma_start(table_sb[:], table)
 
         tpw_sb = held.tile([M, 2, N], F32, name="tpw_sb")
-        nc.scalar.dma_start(tpw_sb[:], tpw.rearrange("(path u) j -> u path j", path=2))
+        nc.sync.dma_start(tpw_sb[:], tpw.rearrange("(path u) j -> u path j", path=2))
         sh_all = held.tile([M, A, N], F32, name="sh_all")
         for first in range(0, A, 2):
-            nc.scalar.dma_start(
+            nc.sync.dma_start(
                 sh_all[:, first : first + 2, :],
                 sh[first : first + 2, :].unsqueeze(0).broadcast_to([M, 2, N]),
             )
 
         w_out_sb = [held.tile([M, M], BF16, name=f"w_out_sb{path}") for path in range(2)]
         nc.sync.dma_start(w_out_sb[0][:], w_out_s)
-        nc.scalar.dma_start(w_out_sb[1][:], w_out_v)
-
-        factor = held.tile([M, A, N], F32, name="factor")
-        for i in range(A):
-            path = min(i, 1)
-            nc.vector.scalar_tensor_tensor(
-                factor[:, i, :], tpw_sb[:, path, :], PATH_SCALE[path], sh_all[:, i, :], MULT, MULT
-            )
+        nc.sync.dma_start(w_out_sb[1][:], w_out_v)
 
         ss_raw = psum.tile([M, N], F32, name="ss_raw")
         nc.tensor.matmul(ss_raw[:], w_up_sb[:], table_sb[:].indirect(offsets[:]), start=True, stop=True)
 
+        weighted = held.tile([M, 2, N], F32, name="weighted")
+        for path in range(2):
+            nc.vector.scalar_tensor_tensor(
+                weighted[:, path, :], ss_raw[:], PATH_SCALE[path], tpw_sb[:, path, :], MULT, MULT
+            )
+
         for i in range(A):
             path = min(i, 1)
             a_i = held.tile([M, N], BF16, name=f"a_{i}")
-            nc.vector.tensor_tensor(a_i[:], ss_raw[:], factor[:, i, :], MULT)
+            nc.vector.tensor_tensor(a_i[:], weighted[:, path, :], sh_all[:, i, :], MULT)
             mixed = psum.tile([M, N], F32, name=f"mixed{i}")
             nc.tensor.matmul(mixed[:], w_out_sb[path][:], a_i[:], start=True, stop=True)
             message = held.tile([M, N], F32, name=f"message{i}")

@@ -4,7 +4,6 @@ import concourse.mybir as mybir
 
 BF16, F32, U16 = mybir.dt.bfloat16, mybir.dt.float32, mybir.dt.uint16
 MULT = mybir.AluOpType.mult
-COPY = mybir.ActivationFunctionType.Copy
 
 D = 128
 M = 128
@@ -56,12 +55,14 @@ def tile_maceedgemessageblock_kernel(tc, table, w_up, tpw, sh, w_out_s, w_out_v,
                 weighted[:, path, :], ss_raw[:], PATH_SCALE[path], tpw_sb[:, path, :], MULT, MULT
             )
 
+        mixed = [psum.tile([M, N], F32, name=f"mixed{i}") for i in range(A)]
         for i in range(A):
             path = min(i, 1)
             a_i = held.tile([M, N], BF16, name=f"a_{i}")
             nc.vector.tensor_tensor(a_i[:], weighted[:, path, :], sh_all[:, i, :], MULT)
-            mixed = psum.tile([M, N], F32, name=f"mixed{i}")
-            nc.tensor.matmul(mixed[:], w_out_sb[path][:], a_i[:], start=True, stop=True)
+            nc.tensor.matmul(mixed[i][:], w_out_sb[path][:], a_i[:], start=True, stop=True)
+
+        for i in range(A):
             message = held.tile([M, N], F32, name=f"message{i}")
-            nc.scalar.activation(message[:], mixed[:], COPY, scale=OUT_SCALE)
+            nc.vector.tensor_scalar_mul(message[:], mixed[i][:], OUT_SCALE)
             nc.sync.dma_start(out[i * M : (i + 1) * M, :], message[:])

@@ -26,12 +26,12 @@ def tile_maceedgemessageblock_kernel(tc, table, w_up, tpw, sh, w_out_s, w_out_v,
         tc.tile_pool(name="held", bufs=1) as held,
         tc.psum_pool(name="psum", bufs=1) as psum,
     ):
+        table_sb = held.tile([D, S], BF16, name="table_sb")
+        nc.sync.dma_start(table_sb[:], table)
         w_up_sb = held.tile([D, M], BF16, name="w_up_sb")
         nc.sync.dma_start(w_up_sb[:], w_up)
         offsets = held.tile([128, N // 16], U16, name="offsets")
         nc.sync.dma_start(offsets[:], offs)
-        table_sb = held.tile([D, S], BF16, name="table_sb")
-        nc.sync.dma_start(table_sb[:], table)
 
         tpw_sb = held.tile([M, 2, N], F32, name="tpw_sb")
         nc.sync.dma_start(tpw_sb[:], tpw.rearrange("(path u) j -> u path j", path=2))

@@ -11,11 +11,11 @@ S = 1024
 N = 128
 A = 4
 
-PATH_SCALE = (
-    math.sqrt(0.5) / math.sqrt(D),
-    math.sqrt(1.5) / math.sqrt(3.0) / math.sqrt(D),
-)
 OUT_SCALE = 1.0 / math.sqrt(2 * M)
+PATH_SCALE = (
+    math.sqrt(0.5) / math.sqrt(D) * OUT_SCALE,
+    math.sqrt(1.5) / math.sqrt(3.0) / math.sqrt(D) * OUT_SCALE,
+)
 
 FLOPS = 2 * D * M * N + A * 2 * M * M * N
 
@@ -64,5 +64,5 @@ def tile_maceedgemessageblock_kernel(tc, table, w_up, tpw, sh, w_out_s, w_out_v,
 
         for i in range(A):
             message = held.tile([M, N], F32, name=f"message{i}")
-            nc.vector.tensor_scalar_mul(message[:], mixed[i][:], OUT_SCALE)
+            nc.vector.tensor_copy(message[:], mixed[i][:])
             nc.sync.dma_start(out[i * M : (i + 1) * M, :], message[:])

import math

import concourse.mybir as mybir

BF16, F32, U16 = mybir.dt.bfloat16, mybir.dt.float32, mybir.dt.uint16
MULT = mybir.AluOpType.mult

D = 128
M = 128
S = 1024
N = 128
A = 4

OUT_SCALE = 1.0 / math.sqrt(2 * M)
PATH_SCALE = (
    math.sqrt(0.5) / math.sqrt(D) * OUT_SCALE,
    math.sqrt(1.5) / math.sqrt(3.0) / math.sqrt(D) * OUT_SCALE,
)

FLOPS = 2 * D * M * N + A * 2 * M * M * N


def tile_maceedgemessageblock_kernel(tc, table, w_up, tpw, sh, w_out_s, w_out_v, offs, out):
    nc = tc.nc
    with (
        tc.tile_pool(name="held", bufs=1) as held,
        tc.psum_pool(name="psum", bufs=1) as psum,
    ):
        table_sb = held.tile([D, S], BF16, name="table_sb")
        nc.sync.dma_start(table_sb[:], table)
        w_up_sb = held.tile([D, M], BF16, name="w_up_sb")
        nc.sync.dma_start(w_up_sb[:], w_up)
        offsets = held.tile([128, N // 16], U16, name="offsets")
        nc.sync.dma_start(offsets[:], offs)

        tpw_sb = held.tile([M, 2, N], F32, name="tpw_sb")
        nc.sync.dma_start(tpw_sb[:], tpw.rearrange("(path u) j -> u path j", path=2))
        sh_all = held.tile([M, A, N], F32, name="sh_all")
        for first in range(0, A, 2):
            nc.sync.dma_start(
                sh_all[:, first : first + 2, :],
                sh[first : first + 2, :].unsqueeze(0).broadcast_to([M, 2, N]),
            )

        w_out_sb = [held.tile([M, M], BF16, name=f"w_out_sb{path}") for path in range(2)]
        nc.sync.dma_start(w_out_sb[0][:], w_out_s)
        nc.sync.dma_start(w_out_sb[1][:], w_out_v)

        ss_raw = psum.tile([M, N], F32, name="ss_raw")
        nc.tensor.matmul(ss_raw[:], w_up_sb[:], table_sb[:].indirect(offsets[:]), start=True, stop=True)

        weighted = held.tile([M, 2, N], F32, name="weighted")
        for path in range(2):
            nc.vector.scalar_tensor_tensor(
                weighted[:, path, :], ss_raw[:], PATH_SCALE[path], tpw_sb[:, path, :], MULT, MULT
            )

        mixed = [psum.tile([M, N], F32, name=f"mixed{i}") for i in range(A)]
        for i in range(A):
            path = min(i, 1)
            a_i = held.tile([M, N], BF16, name=f"a_{i}")
            nc.vector.tensor_tensor(a_i[:], weighted[:, path, :], sh_all[:, i, :], MULT)
            nc.tensor.matmul(mixed[i][:], w_out_sb[path][:], a_i[:], start=True, stop=True)

        for i in range(A):
            message = held.tile([M, N], F32, name=f"message{i}")
            nc.vector.tensor_copy(message[:], mixed[i][:])
            nc.sync.dma_start(out[i * M : (i + 1) * M, :], message[:])
